import numpy as np
import ml_dtypes


def mxq(x, axis, fmt="e4m3"):
    dtype, down = {"e4m3": (ml_dtypes.float8_e4m3fn, 7), "e5m2": (ml_dtypes.float8_e5m2, 14)}[fmt]
    v = np.moveaxis(np.asarray(x, np.float32).astype(ml_dtypes.bfloat16).astype(np.float64), axis, -1)
    blocks = v.reshape(v.shape[:-1] + (-1, 32))
    amax = np.abs(blocks).max(-1, keepdims=True)
    byte = np.maximum(np.where(amax > 0, np.frexp(amax)[1] - 1 + 127, 0) - down, 1)
    scale = np.exp2(byte - 127.0)
    codes = (blocks / scale).astype(np.float32).astype(dtype).astype(np.float64)
    return np.moveaxis((codes * scale).reshape(v.shape), -1, axis)


WIDE = False


def mx_kscale(k):
    if not WIDE:
        return np.ones(k)
    levels = np.array([10, -10, 5, -5, 0])
    a = np.random.permutation(np.resize(levels, k // 512 * 4)).reshape(k // 512, 4)
    idx = np.arange(k)
    return np.exp2(a[idx // 512, idx % 128 // 32])


BF16 = ml_dtypes.bfloat16


def bf(x):
    return np.asarray(x, np.float32).astype(BF16)


def f64(x):
    return np.asarray(x).astype(np.float64)


E2M1 = np.array([0.0, 0.5, 1.0, 1.5, 2.0, 3.0, 4.0, 6.0, -0.0, -0.5, -1.0, -1.5, -2.0, -3.0, -4.0, -6.0])


def pack_weight(w, fmt):
    k, n = w.shape
    w = f64(bf(w)).reshape(k // 32, 32, n)
    amax = np.abs(w).max(1)
    if fmt == "e4m3":
        byte = np.frexp(amax)[1] - 1 + 127 - 7
    else:
        mant, ex = np.frexp(amax / 6.0)
        byte = np.where(mant > 0.5, ex, ex - 1) + 127
    byte = np.clip(np.where(amax > 0, byte, 1), 1, 254)
    scaled = (w * np.exp2(127.0 - byte)[:, None, :]).reshape(k, n).astype(np.float32)
    by_word = np.ascontiguousarray(scaled.reshape(k // 512, 128, 4, n).transpose(0, 1, 3, 2))
    if fmt == "e4m3":
        words = by_word.astype(ml_dtypes.float8_e4m3fn).view(np.uint8)
    else:
        c = by_word.astype(ml_dtypes.float4_e2m1fn).view(np.uint8) & 0xF
        words = c[..., 0::2] | (c[..., 1::2] << 4)
    return np.ascontiguousarray(words), np.ascontiguousarray(byte.astype(np.uint8).reshape(k // 512, 16, n))


def unpack_weight(words, scales, fmt):
    g, p, n, _ = words.shape
    if fmt == "e4m3":
        vals = np.ascontiguousarray(words).view(ml_dtypes.float8_e4m3fn).astype(np.float64)
    else:
        nib = np.empty((g, p, n, 4), np.uint8)
        nib[..., 0::2] = words & 0xF
        nib[..., 1::2] = words >> 4
        vals = E2M1[nib]
    vals = vals * np.repeat(np.exp2(scales.astype(np.float64) - 127.0), 8, axis=1)[..., None]
    return vals.transpose(0, 1, 3, 2).reshape(g * 512, n)

def pack4(w):
    words, scales = pack_weight(w, "e2m1")
    return words.reshape(words.shape[0], 128, -1), scales


def unpack4(words, scales):
    return unpack_weight(words.reshape(words.shape[0], 128, -1, 2), scales, "e2m1")


B, T, C, F = 4, 512, 512, 2048
M = T


def silu(v):
    return v / (1.0 + np.exp(-v))


def sigmoid(v):
    return 1.0 / (1.0 + np.exp(-v))


def setup_inputs():
    t = mx_kscale(F)
    x = np.random.standard_normal((B, T, C)) + 0.5 * np.random.standard_normal((B, 1, C))
    h = bf(silu(np.random.standard_normal((B, T, F)) * 0.85) * t)
    memory = bf(np.random.standard_normal((1, M, C)) * 6.0 / np.sqrt(C))
    w2_words, w2_scales = pack4(np.random.standard_normal((F, C)) * 3.0 / np.sqrt(F) / t[:, None])
    b2 = bf(np.random.standard_normal(C) * 0.5)
    return {"h": h,
            "x": bf(x),
            "memory": memory,
            "w2_words": w2_words,
            "w2_scales": w2_scales,
            "b2": b2}


def reference(h, x, memory, w2_words, w2_scales, b2):
    update_gate = sigmoid((mxq(f64(h), 2, "e4m3") @ unpack4(w2_words, w2_scales)) + f64(b2))
    x_mean = f64(x).mean(axis=1, keepdims=True)
    new_mem = f64(memory) * (1.0 - update_gate) + x_mean * update_gate
    return new_mem.mean(axis=0, keepdims=True)

@@ -1,0 +1,227 @@
+from contextlib import ExitStack
+
+import concourse.mybir as mybir
+from concourse.masks import make_identity
+
+F32 = mybir.dt.float32
+BF16 = mybir.dt.bfloat16
+I32 = mybir.dt.int32
+U32 = mybir.dt.uint32
+U8 = mybir.dt.uint8
+FP8X4 = mybir.dt.float8_e4m3fn_x4
+FP4X4 = mybir.dt.float4_e2m1fn_x4
+ALU = mybir.AluOpType
+ACT = mybir.ActivationFunctionType
+
+B, T, C, F = 4, 512, 512, 2048
+P = 128
+PACK = 4
+K_PASS = P * PACK
+PASSES = F // K_PASS
+TOKEN_TILES = T // P
+CHANNEL_TILES = C // P
+STEP_PASSES = 2
+STEP_K = STEP_PASSES * K_PASS
+STEPS_PER_BATCH = PASSES // STEP_PASSES
+STEPS = B * STEPS_PER_BATCH
+PAIR = 2
+PAIRS = TOKEN_TILES // PAIR
+WORDS_PER_PASS = K_PASS // 2
+MEAN_COLS = 32
+
+FLOPS = 2 * B * T * F * C
+
+
+def tile_dynamicmemorybank_pb_kernel(tc, h, x, memory, w2_words, w2_scales, b2, out):
+    nc = tc.nc
+    with ExitStack() as ctx:
+        ctx.enter_context(tc.manual_schedule())
+        keep = ctx.enter_context(tc.tile_pool(name="keep", bufs=1))
+        stage = ctx.enter_context(tc.tile_pool(name="stage", bufs=2))
+        gates = ctx.enter_context(tc.tile_pool(name="gates", bufs=4))
+        plain_psum = ctx.enter_context(tc.psum_pool(name="plain_psum", bufs=4))
+        mx_psum = ctx.enter_context(tc.psum_pool(name="mx_psum", bufs=CHANNEL_TILES))
+
+        ident_f32 = keep.tile([P, P], F32)
+        make_identity(nc, ident_f32[:])
+        ident_bf16 = keep.tile([P, P], BF16)
+        make_identity(nc, ident_bf16[:])
+        w_scales = keep.tile([P, PASSES, C], U8, align_bytes=64)
+        nc.vector.memset(w_scales[:].bitcast(I32), 0)
+        bias_rows = keep.tile([P, P], BF16)
+        nc.vector.memset(bias_rows[:], 0.0)
+        mean_weight = keep.tile([P, MEAN_COLS], BF16)
+        nc.vector.memset(mean_weight[:], -1.0 / (B * T))
+        table_warmer = keep.tile([P, 1], F32)
+        nc.vector.memset(table_warmer[:], 0.0)
+        nc.scalar.activation(out=table_warmer[:], in_=table_warmer[:], func=ACT.Sigmoid)
+
+        h_tiles = {}
+
+        def load_h(step):
+            b, half = divmod(step, STEPS_PER_BATCH)
+            by_tile = h[b].rearrange("(j p) k -> p j k", p=P)
+            for pair in range(PAIRS):
+                h_tile = keep.tile([P, PAIR, STEP_K], BF16, name="h_%d_%d" % (step, pair))
+                nc.sync.dma_start(
+                    out=h_tile[:],
+                    in_=by_tile[:, pair * PAIR : (pair + 1) * PAIR, half * STEP_K : (half + 1) * STEP_K],
+                )
+                h_tiles[(step, pair)] = h_tile
+
+        x_tiles = {}
+
+        def load_x(b):
+            x_tile = keep.tile([P, TOKEN_TILES, C], BF16, name="x_%d" % b)
+            nc.sync.dma_start(
+                out=x_tile[:].rearrange("p j c -> p (j c)"),
+                in_=x[b].rearrange("(p j) c -> p (j c)", j=TOKEN_TILES),
+            )
+            x_tiles[b] = x_tile
+
+        load_h(0)
+        load_h(1)
+        scale_rows = w2_scales.bitcast(I32).rearrange("g (Q r) n -> r Q g n", r=4)
+        for r in range(4):
+            nc.sync.dma_start(out=w_scales[r:P:32, :, :].bitcast(I32), in_=scale_rows[r])
+        w_words = keep.tile([P, PASSES, 2 * C], U8, align_bytes=64)
+        nc.sync.dma_start(out=w_words[:].bitcast(I32), in_=w2_words.bitcast(I32).rearrange("g p n -> p g n"))
+        load_h(2)
+        nc.sync.dma_start(out=bias_rows[0:CHANNEL_TILES, :], in_=b2.rearrange("(r c) -> r c", c=P))
+        mem_rows = keep.tile([P, TOKEN_TILES, C], BF16)
+        nc.sync.dma_start(out=mem_rows[:], in_=memory[0].rearrange("(j p) c -> p j c", p=P))
+        load_x(0)
+        for b in range(1, B):
+            load_h(STEPS_PER_BATCH * b + 1)
+            if b + 1 < B:
+                load_h(STEPS_PER_BATCH * (b + 1))
+            load_x(b)
+
+        def transpose_and_quantise(step):
+            grouped = stage.tile([P, STEP_PASSES, PACK * T], BF16, align_bytes=64)
+            grouped_words = grouped[:].bitcast(F32)
+            for pair in range(PAIRS):
+                h_words = h_tiles[(step, pair)][:].bitcast(F32)
+                for i in range(STEP_PASSES):
+                    bank = plain_psum.tile([P, 2, PAIR * P], F32, tag="bank")
+                    for j in range(PAIR):
+                        for u in range(2):
+                            nc.tensor.transpose(
+                                bank[:, u, j * P : (j + 1) * P],
+                                h_words[:, j, i * WORDS_PER_PASS + u : (i + 1) * WORDS_PER_PASS : 2],
+                                ident_f32[:],
+                            )
+                    first = pair * PAIR * P * 2
+                    nc.scalar.copy(
+                        out=grouped_words[:, i, first : first + PAIR * P * 2].rearrange("p (m u) -> p m u", u=2),
+                        in_=bank[:].rearrange("p u m -> p m u"),
+                    )
+            h_codes = stage.tile([P, STEP_PASSES, T], U32, align_bytes=64)
+            h_scales = stage.tile([P, STEP_PASSES, T], U8, align_bytes=64)
+            for i in range(STEP_PASSES):
+                nc.vector.quantize_mx(
+                    out=h_codes[:, i, :].bitcast(FP8X4), scales=h_scales[:, i, :], in_=grouped[:, i, :]
+                )
+            return h_codes, h_scales
+
+        def multiply(step, products, h_codes, h_scales):
+            first_pass = (step % STEPS_PER_BATCH) * STEP_PASSES
+            for ct in range(CHANNEL_TILES):
+                for i in range(STEP_PASSES):
+                    g = first_pass + i
+                    nc.tensor.matmul_mx(
+                        out=products[ct][:],
+                        lhsT=w_words[:, g, ct * 2 * P : (ct + 1) * 2 * P].bitcast(FP4X4),
+                        lhsT_scale=w_scales[:, g, ct * P : (ct + 1) * P],
+                        rhs=h_codes[:, i, :].bitcast(FP8X4),
+                        rhs_scale=h_scales[:, i, :],
+                        start=(g == 0),
+                        stop=(g == PASSES - 1),
+                    )
+
+        bias = keep.tile([P, CHANNEL_TILES], F32)
+        neg_quarter_mem = [keep.tile([P, T], BF16, name="neg_quarter_mem_%d" % ct) for ct in range(CHANNEL_TILES)]
+
+        def transpose_bias_and_memory():
+            bias_bank = plain_psum.tile([P, P], BF16, tag="bank")
+            nc.tensor.transpose(bias_bank[:], bias_rows[:], ident_bf16[:])
+            nc.vector.tensor_copy(out=bias[:], in_=bias_bank[:, 0:CHANNEL_TILES])
+            for ct in range(CHANNEL_TILES):
+                mem_bank = plain_psum.tile([P, T], BF16, tag="bank")
+                for j in range(TOKEN_TILES):
+                    nc.tensor.transpose(
+                        mem_bank[:, j * P : (j + 1) * P], mem_rows[:, j, ct * P : (ct + 1) * P], ident_bf16[:]
+                    )
+                nc.vector.tensor_scalar_mul(out=neg_quarter_mem[ct][:], in0=mem_bank[:], scalar1=-0.25)
+
+        def token_mean(b):
+            sums = plain_psum.tile([P, CHANNEL_TILES, MEAN_COLS], F32, tag="bank")
+            for ct in range(CHANNEL_TILES):
+                for j in range(TOKEN_TILES):
+                    nc.tensor.matmul(
+                        out=sums[:, ct, :],
+                        lhsT=x_tiles[b][:, j, ct * P : (ct + 1) * P],
+                        rhs=mean_weight[:],
+                        start=(j == 0),
+                        stop=(j == TOKEN_TILES - 1),
+                    )
+            neg_quarter_mean = keep.tile([P, CHANNEL_TILES], F32, name="neg_quarter_mean_%d" % b)
+            nc.vector.tensor_copy(out=neg_quarter_mean[:], in_=sums[:, :, 0])
+            return neg_quarter_mean
+
+        blended = [keep.tile([P, T], F32, name="blended_%d" % ct) for ct in range(CHANNEL_TILES)]
+
+        def gate_and_blend(b, products, neg_quarter_mean):
+            for ct in range(CHANNEL_TILES):
+                gate = gates.tile([P, T], F32)
+                nc.scalar.activation(
+                    out=gate[:], in_=products[ct][:], func=ACT.Sigmoid, bias=bias[:, ct : ct + 1], scale=1.0
+                )
+                pull = gates.tile([P, T], F32)
+                nc.vector.scalar_tensor_tensor(
+                    out=pull[:],
+                    in0=neg_quarter_mem[ct][:],
+                    scalar=neg_quarter_mean[:, ct : ct + 1],
+                    in1=gate[:],
+                    op0=ALU.subtract,
+                    op1=ALU.mult,
+                )
+                if b == 0:
+                    nc.vector.scalar_tensor_tensor(
+                        out=blended[ct][:],
+                        in0=neg_quarter_mem[ct][:],
+                        scalar=-4.0,
+                        in1=pull[:],
+                        op0=ALU.mult,
+                        op1=ALU.add,
+                    )
+                else:
+                    nc.vector.tensor_tensor(out=blended[ct][:], in0=blended[ct][:], in1=pull[:], op=ALU.add)
+
+        quantised = {0: transpose_and_quantise(0)}
+        products = None
+        for step in range(STEPS):
+            b, half = divmod(step, STEPS_PER_BATCH)
+            last_of_batch = half == STEPS_PER_BATCH - 1
+            if step + 1 < STEPS:
+                quantised[step + 1] = transpose_and_quantise(step + 1)
+            if step == STEPS_PER_BATCH - 1:
+                transpose_bias_and_memory()
+            if last_of_batch:
+                neg_quarter_mean = token_mean(b)
+            if half == 0:
+                products = [mx_psum.tile([P, T], F32, name="product_%d" % ct, tag="product") for ct in range(CHANNEL_TILES)]
+            h_codes, h_scales = quantised[step]
+            multiply(step, products, h_codes, h_scales)
+            if last_of_batch:
+                gate_and_blend(b, products, neg_quarter_mean)
+
+        out_rows = keep.tile([P, TOKEN_TILES, C], F32)
+        out_by_tile = out[0].rearrange("(j p) c -> p j c", p=P)
+        for ct in range(CHANNEL_TILES):
+            back = plain_psum.tile([P, TOKEN_TILES, P], F32, tag="bank")
+            for j in range(TOKEN_TILES):
+                nc.tensor.transpose(back[:, j, :], blended[ct][:, j * P : (j + 1) * P], ident_f32[:])
+            channels = slice(ct * P, (ct + 1) * P)
+            nc.scalar.copy(out=out_rows[:, :, channels], in_=back[:])
+            nc.sync.dma_start(out=out_by_tile[:, :, channels], in_=out_rows[:, :, channels])

@@ -24,6 +24,8 @@ STEP_PASSES = 2
 STEP_K = STEP_PASSES * K_PASS
 STEPS_PER_BATCH = PASSES // STEP_PASSES
 STEPS = B * STEPS_PER_BATCH
+LEAD = STEPS_PER_BATCH + 1
+RUN_TILES = CHANNEL_TILES // STEPS_PER_BATCH
 PAIR = 2
 PAIRS = TOKEN_TILES // PAIR
 WORDS_PER_PASS = K_PASS // 2
@@ -38,9 +40,10 @@ def tile_dynamicmemorybank_pb_kernel(tc, h, x, memory, w2_words, w2_scales, b2, 
         ctx.enter_context(tc.manual_schedule())
         keep = ctx.enter_context(tc.tile_pool(name="keep", bufs=1))
         stage = ctx.enter_context(tc.tile_pool(name="stage", bufs=2))
+        mx_h = ctx.enter_context(tc.tile_pool(name="mx_h", bufs=2 * STEPS_PER_BATCH))
         gates = ctx.enter_context(tc.tile_pool(name="gates", bufs=4))
-        plain_psum = ctx.enter_context(tc.psum_pool(name="plain_psum", bufs=4))
-        mx_psum = ctx.enter_context(tc.psum_pool(name="mx_psum", bufs=CHANNEL_TILES))
+        mx_psum = ctx.enter_context(tc.psum_pool(name="mx_psum", bufs=2))
+        plain_psum = ctx.enter_context(tc.psum_pool(name="plain_psum", bufs=6))
 
         ident_f32 = keep.tile([P, P], F32)
         make_identity(nc, ident_f32[:])
@@ -79,25 +82,23 @@ def tile_dynamicmemorybank_pb_kernel(tc, h, x, memory, w2_words, w2_scales, b2, 
             )
             x_tiles[b] = x_tile
 
-        load_h(0)
-        load_h(1)
+        for step in range(LEAD):
+            load_h(step)
         scale_rows = w2_scales.bitcast(I32).rearrange("g (Q r) n -> r Q g n", r=4)
         for r in range(4):
             nc.sync.dma_start(out=w_scales[r:P:32, :, :].bitcast(I32), in_=scale_rows[r])
         w_words = keep.tile([P, PASSES, 2 * C], U8, align_bytes=64)
         nc.sync.dma_start(out=w_words[:].bitcast(I32), in_=w2_words.bitcast(I32).rearrange("g p n -> p g n"))
-        load_h(2)
         nc.sync.dma_start(out=bias_rows[0:CHANNEL_TILES, :], in_=b2.rearrange("(r c) -> r c", c=P))
         mem_rows = keep.tile([P, TOKEN_TILES, C], BF16)
         nc.sync.dma_start(out=mem_rows[:], in_=memory[0].rearrange("(j p) c -> p j c", p=P))
         load_x(0)
-        for b in range(1, B):
-            load_h(STEPS_PER_BATCH * b + 1)
-            if b + 1 < B:
-                load_h(STEPS_PER_BATCH * (b + 1))
-            load_x(b)
+        for step in range(LEAD, STEPS):
+            load_h(step)
+            if step % STEPS_PER_BATCH == STEPS_PER_BATCH - 1:
+                load_x(step // STEPS_PER_BATCH)
 
-        def transpose_and_quantise(step):
+        def transpose(step):
             grouped = stage.tile([P, STEP_PASSES, PACK * T], BF16, align_bytes=64)
             grouped_words = grouped[:].bitcast(F32)
             for pair in range(PAIRS):
@@ -116,28 +117,34 @@ def tile_dynamicmemorybank_pb_kernel(tc, h, x, memory, w2_words, w2_scales, b2, 
                         out=grouped_words[:, i, first : first + PAIR * P * 2].rearrange("p (m u) -> p m u", u=2),
                         in_=bank[:].rearrange("p u m -> p m u"),
                     )
-            h_codes = stage.tile([P, STEP_PASSES, T], U32, align_bytes=64)
-            h_scales = stage.tile([P, STEP_PASSES, T], U8, align_bytes=64)
+            return grouped
+
+        quantised = {}
+
+        def quantise(step, grouped):
+            h_codes = mx_h.tile([P, STEP_PASSES, T], U32, align_bytes=64)
+            h_scales = mx_h.tile([P, STEP_PASSES, T], U8, align_bytes=64)
             for i in range(STEP_PASSES):
                 nc.vector.quantize_mx(
                     out=h_codes[:, i, :].bitcast(FP8X4), scales=h_scales[:, i, :], in_=grouped[:, i, :]
                 )
-            return h_codes, h_scales
+            quantised[step] = (h_codes, h_scales)
 
-        def multiply(step, products, h_codes, h_scales):
-            first_pass = (step % STEPS_PER_BATCH) * STEP_PASSES
-            for ct in range(CHANNEL_TILES):
-                for i in range(STEP_PASSES):
-                    g = first_pass + i
-                    nc.tensor.matmul_mx(
-                        out=products[ct][:],
-                        lhsT=w_words[:, g, ct * 2 * P : (ct + 1) * 2 * P].bitcast(FP4X4),
-                        lhsT_scale=w_scales[:, g, ct * P : (ct + 1) * P],
-                        rhs=h_codes[:, i, :].bitcast(FP8X4),
-                        rhs_scale=h_scales[:, i, :],
-                        start=(g == 0),
-                        stop=(g == PASSES - 1),
-                    )
+        def multiply(b, ct):
+            product = mx_psum.tile([P, T], F32)
+            for g in range(PASSES):
+                h_codes, h_scales = quantised[b * STEPS_PER_BATCH + g // STEP_PASSES]
+                i = g % STEP_PASSES
+                nc.tensor.matmul_mx(
+                    out=product[:],
+                    lhsT=w_words[:, g, ct * 2 * P : (ct + 1) * 2 * P].bitcast(FP4X4),
+                    lhsT_scale=w_scales[:, g, ct * P : (ct + 1) * P],
+                    rhs=h_codes[:, i, :].bitcast(FP8X4),
+                    rhs_scale=h_scales[:, i, :],
+                    start=(g == 0),
+                    stop=(g == PASSES - 1),
+                )
+            return product
 
         bias = keep.tile([P, CHANNEL_TILES], F32)
         neg_quarter_mem = [keep.tile([P, T], BF16, name="neg_quarter_mem_%d" % ct) for ct in range(CHANNEL_TILES)]
@@ -154,6 +161,8 @@ def tile_dynamicmemorybank_pb_kernel(tc, h, x, memory, w2_words, w2_scales, b2, 
                     )
                 nc.vector.tensor_scalar_mul(out=neg_quarter_mem[ct][:], in0=mem_bank[:], scalar1=-0.25)
 
+        neg_quarter_means = {}
+
         def token_mean(b):
             sums = plain_psum.tile([P, CHANNEL_TILES, MEAN_COLS], F32, tag="bank")
             for ct in range(CHANNEL_TILES):
@@ -167,54 +176,53 @@ def tile_dynamicmemorybank_pb_kernel(tc, h, x, memory, w2_words, w2_scales, b2, 
                     )
             neg_quarter_mean = keep.tile([P, CHANNEL_TILES], F32, name="neg_quarter_mean_%d" % b)
             nc.vector.tensor_copy(out=neg_quarter_mean[:], in_=sums[:, :, 0])
-            return neg_quarter_mean
+            neg_quarter_means[b] = neg_quarter_mean
 
         blended = [keep.tile([P, T], F32, name="blended_%d" % ct) for ct in range(CHANNEL_TILES)]
 
-        def gate_and_blend(b, products, neg_quarter_mean):
-            for ct in range(CHANNEL_TILES):
-                gate = gates.tile([P, T], F32)
-                nc.scalar.activation(
-                    out=gate[:], in_=products[ct][:], func=ACT.Sigmoid, bias=bias[:, ct : ct + 1], scale=1.0
-                )
-                pull = gates.tile([P, T], F32)
+        def gate_and_blend(b, ct, product):
+            gate = gates.tile([P, T], F32)
+            nc.scalar.activation(
+                out=gate[:], in_=product[:], func=ACT.Sigmoid, bias=bias[:, ct : ct + 1], scale=1.0
+            )
+            pull = gates.tile([P, T], F32)
+            nc.vector.scalar_tensor_tensor(
+                out=pull[:],
+                in0=neg_quarter_mem[ct][:],
+                scalar=neg_quarter_means[b][:, ct : ct + 1],
+                in1=gate[:],
+                op0=ALU.subtract,
+                op1=ALU.mult,
+            )
+            if b == 0:
                 nc.vector.scalar_tensor_tensor(
-                    out=pull[:],
+                    out=blended[ct][:],
                     in0=neg_quarter_mem[ct][:],
-                    scalar=neg_quarter_mean[:, ct : ct + 1],
-                    in1=gate[:],
-                    op0=ALU.subtract,
-                    op1=ALU.mult,
+                    scalar=-4.0,
+                    in1=pull[:],
+                    op0=ALU.mult,
+                    op1=ALU.add,
                 )
-                if b == 0:
-                    nc.vector.scalar_tensor_tensor(
-                        out=blended[ct][:],
-                        in0=neg_quarter_mem[ct][:],
-                        scalar=-4.0,
-                        in1=pull[:],
-                        op0=ALU.mult,
-                        op1=ALU.add,
-                    )
-                else:
-                    nc.vector.tensor_tensor(out=blended[ct][:], in0=blended[ct][:], in1=pull[:], op=ALU.add)
+            else:
+                nc.vector.tensor_tensor(out=blended[ct][:], in0=blended[ct][:], in1=pull[:], op=ALU.add)
 
-        quantised = {0: transpose_and_quantise(0)}
-        products = None
-        for step in range(STEPS):
-            b, half = divmod(step, STEPS_PER_BATCH)
-            last_of_batch = half == STEPS_PER_BATCH - 1
-            if step + 1 < STEPS:
-                quantised[step + 1] = transpose_and_quantise(step + 1)
-            if step == STEPS_PER_BATCH - 1:
-                transpose_bias_and_memory()
-            if last_of_batch:
-                neg_quarter_mean = token_mean(b)
-            if half == 0:
-                products = [mx_psum.tile([P, T], F32, name="product_%d" % ct, tag="product") for ct in range(CHANNEL_TILES)]
-            h_codes, h_scales = quantised[step]
-            multiply(step, products, h_codes, h_scales)
-            if last_of_batch:
-                gate_and_blend(b, products, neg_quarter_mean)
+        for step in range(STEPS_PER_BATCH):
+            quantise(step, transpose(step))
+        for b in range(B):
+            for run in range(STEPS_PER_BATCH):
+                ahead = (b + 1) * STEPS_PER_BATCH + run
+                if ahead < STEPS:
+                    grouped = transpose(ahead)
+                    if run == STEPS_PER_BATCH - 1:
+                        token_mean(b + 1)
+                    quantise(ahead, grouped)
+                tiles = range(run * RUN_TILES, (run + 1) * RUN_TILES)
+                products = [multiply(b, ct) for ct in tiles]
+                if b == 0 and run == 0:
+                    transpose_bias_and_memory()
+                    token_mean(0)
+                for ct, product in zip(tiles, products):
+                    gate_and_blend(b, ct, product)
 
         out_rows = keep.tile([P, TOKEN_TILES, C], F32)
         out_by_tile = out[0].rearrange("(j p) c -> p j c", p=P)

@@ -37,7 +37,6 @@ FLOPS = 2 * B * T * F * C
 def tile_dynamicmemorybank_pb_kernel(tc, h, x, memory, w2_words, w2_scales, b2, out):
     nc = tc.nc
     with ExitStack() as ctx:
-        ctx.enter_context(tc.manual_schedule())
         keep = ctx.enter_context(tc.tile_pool(name="keep", bufs=1))
         stage = ctx.enter_context(tc.tile_pool(name="stage", bufs=2))
         mx_h = ctx.enter_context(tc.tile_pool(name="mx_h", bufs=2 * STEPS_PER_BATCH))

@@ -20,14 +20,13 @@ K_PASS = P * PACK
 PASSES = F // K_PASS
 TOKEN_TILES = T // P
 CHANNEL_TILES = C // P
-STEP_PASSES = 2
-STEP_K = STEP_PASSES * K_PASS
-STEPS_PER_BATCH = PASSES // STEP_PASSES
+STEP_TILES = 2
+STEP_TOKENS = STEP_TILES * P
+STEPS_PER_BATCH = TOKEN_TILES // STEP_TILES
 STEPS = B * STEPS_PER_BATCH
 LEAD = STEPS_PER_BATCH + 1
 RUN_TILES = CHANNEL_TILES // STEPS_PER_BATCH
-PAIR = 2
-PAIRS = TOKEN_TILES // PAIR
+BANK_PASSES = 2
 WORDS_PER_PASS = K_PASS // 2
 MEAN_COLS = 32
 
@@ -39,7 +38,7 @@ def tile_dynamicmemorybank_pb_kernel(tc, h, x, memory, w2_words, w2_scales, b2, 
     with ExitStack() as ctx:
         keep = ctx.enter_context(tc.tile_pool(name="keep", bufs=1))
         stage = ctx.enter_context(tc.tile_pool(name="stage", bufs=2))
-        mx_h = ctx.enter_context(tc.tile_pool(name="mx_h", bufs=2 * STEPS_PER_BATCH))
+        mx_h = ctx.enter_context(tc.tile_pool(name="mx_h", bufs=2))
         gates = ctx.enter_context(tc.tile_pool(name="gates", bufs=4))
         mx_psum = ctx.enter_context(tc.psum_pool(name="mx_psum", bufs=2))
         plain_psum = ctx.enter_context(tc.psum_pool(name="plain_psum", bufs=6))
@@ -62,14 +61,11 @@ def tile_dynamicmemorybank_pb_kernel(tc, h, x, memory, w2_words, w2_scales, b2, 
 
         def load_h(step):
             b, half = divmod(step, STEPS_PER_BATCH)
-            by_tile = h[b].rearrange("(j p) k -> p j k", p=P)
-            for pair in range(PAIRS):
-                h_tile = keep.tile([P, PAIR, STEP_K], BF16, name="h_%d_%d" % (step, pair))
-                nc.sync.dma_start(
-                    out=h_tile[:],
-                    in_=by_tile[:, pair * PAIR : (pair + 1) * PAIR, half * STEP_K : (half + 1) * STEP_K],
-                )
-                h_tiles[(step, pair)] = h_tile
+            for j in range(STEP_TILES):
+                first_token = (half * STEP_TILES + j) * P
+                h_tile = keep.tile([P, F], BF16, name="h_%d_%d" % (step, j))
+                nc.sync.dma_start(out=h_tile[:], in_=h[b, first_token : first_token + P, :])
+                h_tiles[(step, j)] = h_tile
 
         x_tiles = {}
 
@@ -98,48 +94,53 @@ def tile_dynamicmemorybank_pb_kernel(tc, h, x, memory, w2_words, w2_scales, b2, 
                 load_x(step // STEPS_PER_BATCH)
 
         def transpose(step):
-            grouped = stage.tile([P, STEP_PASSES, PACK * T], BF16, align_bytes=64)
+            grouped = stage.tile([P, PASSES, PACK * STEP_TOKENS], BF16, align_bytes=64)
             grouped_words = grouped[:].bitcast(F32)
-            for pair in range(PAIRS):
-                h_words = h_tiles[(step, pair)][:].bitcast(F32)
-                for i in range(STEP_PASSES):
-                    bank = plain_psum.tile([P, 2, PAIR * P], F32, tag="bank")
-                    for j in range(PAIR):
+            for j in range(STEP_TILES):
+                h_words = h_tiles[(step, j)][:].bitcast(F32)
+                for first_pass in range(0, PASSES, BANK_PASSES):
+                    bank = plain_psum.tile([P, BANK_PASSES, 2, P], F32, tag="bank")
+                    for i in range(BANK_PASSES):
+                        g = first_pass + i
                         for u in range(2):
                             nc.tensor.transpose(
-                                bank[:, u, j * P : (j + 1) * P],
-                                h_words[:, j, i * WORDS_PER_PASS + u : (i + 1) * WORDS_PER_PASS : 2],
+                                bank[:, i, u, :],
+                                h_words[:, g * WORDS_PER_PASS + u : (g + 1) * WORDS_PER_PASS : 2],
                                 ident_f32[:],
                             )
-                    first = pair * PAIR * P * 2
                     nc.scalar.copy(
-                        out=grouped_words[:, i, first : first + PAIR * P * 2].rearrange("p (m u) -> p m u", u=2),
-                        in_=bank[:].rearrange("p u m -> p m u"),
+                        out=grouped_words[
+                            :, first_pass : first_pass + BANK_PASSES, j * 2 * P : (j + 1) * 2 * P
+                        ].rearrange("p g (m u) -> p g m u", u=2),
+                        in_=bank[:].rearrange("p g u m -> p g m u"),
                     )
             return grouped
 
         quantised = {}
 
         def quantise(step, grouped):
-            h_codes = mx_h.tile([P, STEP_PASSES, T], U32, align_bytes=64)
-            h_scales = mx_h.tile([P, STEP_PASSES, T], U8, align_bytes=64)
-            for i in range(STEP_PASSES):
+            b, half = divmod(step, STEPS_PER_BATCH)
+            if half == 0:
+                h_codes = mx_h.tile([P, PASSES, T], U32, align_bytes=64)
+                h_scales = mx_h.tile([P, PASSES, T], U8, align_bytes=64)
+                quantised[b] = (h_codes, h_scales)
+            h_codes, h_scales = quantised[b]
+            tokens = slice(half * STEP_TOKENS, (half + 1) * STEP_TOKENS)
+            for g in range(PASSES):
                 nc.vector.quantize_mx(
-                    out=h_codes[:, i, :].bitcast(FP8X4), scales=h_scales[:, i, :], in_=grouped[:, i, :]
+                    out=h_codes[:, g, tokens].bitcast(FP8X4), scales=h_scales[:, g, tokens], in_=grouped[:, g, :]
                 )
-            quantised[step] = (h_codes, h_scales)
 
         def multiply(b, ct):
             product = mx_psum.tile([P, T], F32)
+            h_codes, h_scales = quantised[b]
             for g in range(PASSES):
-                h_codes, h_scales = quantised[b * STEPS_PER_BATCH + g // STEP_PASSES]
-                i = g % STEP_PASSES
                 nc.tensor.matmul_mx(
                     out=product[:],
                     lhsT=w_words[:, g, ct * 2 * P : (ct + 1) * 2 * P].bitcast(FP4X4),
                     lhsT_scale=w_scales[:, g, ct * P : (ct + 1) * P],
-                    rhs=h_codes[:, i, :].bitcast(FP8X4),
-                    rhs_scale=h_scales[:, i, :],
+                    rhs=h_codes[:, g, :].bitcast(FP8X4),
+                    rhs_scale=h_scales[:, g, :],
                     start=(g == 0),
                     stop=(g == PASSES - 1),
                 )

@@ -38,6 +38,7 @@ def tile_dynamicmemorybank_pb_kernel(tc, h, x, memory, w2_words, w2_scales, b2, 
     with ExitStack() as ctx:
         keep = ctx.enter_context(tc.tile_pool(name="keep", bufs=1))
         stage = ctx.enter_context(tc.tile_pool(name="stage", bufs=2))
+        ordered = ctx.enter_context(tc.tile_pool(name="ordered", bufs=2 * STEP_TILES))
         mx_h = ctx.enter_context(tc.tile_pool(name="mx_h", bufs=2))
         gates = ctx.enter_context(tc.tile_pool(name="gates", bufs=4))
         mx_psum = ctx.enter_context(tc.psum_pool(name="mx_psum", bufs=2))
@@ -52,7 +53,7 @@ def tile_dynamicmemorybank_pb_kernel(tc, h, x, memory, w2_words, w2_scales, b2, 
         bias_rows = keep.tile([P, P], BF16)
         nc.vector.memset(bias_rows[:], 0.0)
         mean_weight = keep.tile([P, MEAN_COLS], BF16)
-        nc.vector.memset(mean_weight[:], -1.0 / (B * T))
+        nc.vector.memset(mean_weight[:], 1.0 / (B * T))
         table_warmer = keep.tile([P, 1], F32)
         nc.vector.memset(table_warmer[:], 0.0)
         nc.scalar.activation(out=table_warmer[:], in_=table_warmer[:], func=ACT.Sigmoid)
@@ -93,6 +94,17 @@ def tile_dynamicmemorybank_pb_kernel(tc, h, x, memory, w2_words, w2_scales, b2, 
             if step % STEPS_PER_BATCH == STEPS_PER_BATCH - 1:
                 load_x(step // STEPS_PER_BATCH)
 
+        regrouped = {}
+
+        def regroup(step):
+            for j in range(STEP_TILES):
+                by_half = ordered.tile([P, PASSES, 2, P], F32, name="by_half")
+                nc.vector.tensor_copy(
+                    out=by_half[:],
+                    in_=h_tiles[(step, j)][:].bitcast(F32).rearrange("p (g m u) -> p g u m", g=PASSES, u=2),
+                )
+                regrouped[(step, j)] = by_half
+
         def transpose(step):
             grouped = stage.tile([P, PASSES, PACK * STEP_TOKENS], BF16, align_bytes=64)
             grouped_words = grouped[:].bitcast(F32)
@@ -103,11 +115,11 @@ def tile_dynamicmemorybank_pb_kernel(tc, h, x, memory, w2_words, w2_scales, b2, 
                     for i in range(BANK_PASSES):
                         g = first_pass + i
                         for u in range(2):
-                            nc.tensor.transpose(
-                                bank[:, i, u, :],
-                                h_words[:, g * WORDS_PER_PASS + u : (g + 1) * WORDS_PER_PASS : 2],
-                                ident_f32[:],
-                            )
+                            if (step, j) in regrouped:
+                                words = regrouped[(step, j)][:, g, u, :]
+                            else:
+                                words = h_words[:, g * WORDS_PER_PASS + u : (g + 1) * WORDS_PER_PASS : 2]
+                            nc.tensor.transpose(bank[:, i, u, :], words, ident_f32[:])
                     nc.scalar.copy(
                         out=grouped_words[
                             :, first_pass : first_pass + BANK_PASSES, j * 2 * P : (j + 1) * 2 * P
@@ -146,22 +158,23 @@ def tile_dynamicmemorybank_pb_kernel(tc, h, x, memory, w2_words, w2_scales, b2, 
                 )
             return product
 
-        bias = keep.tile([P, CHANNEL_TILES], F32)
-        neg_quarter_mem = [keep.tile([P, T], BF16, name="neg_quarter_mem_%d" % ct) for ct in range(CHANNEL_TILES)]
+        neg_bias = keep.tile([P, CHANNEL_TILES], F32)
+        quarter_mem = [keep.tile([P, T], BF16, name="quarter_mem_%d" % ct) for ct in range(CHANNEL_TILES)]
 
         def transpose_bias_and_memory():
             bias_bank = plain_psum.tile([P, P], BF16, tag="bank")
             nc.tensor.transpose(bias_bank[:], bias_rows[:], ident_bf16[:])
-            nc.vector.tensor_copy(out=bias[:], in_=bias_bank[:, 0:CHANNEL_TILES])
+            nc.vector.tensor_scalar_mul(out=neg_bias[:], in0=bias_bank[:, 0:CHANNEL_TILES], scalar1=-1.0)
             for ct in range(CHANNEL_TILES):
                 mem_bank = plain_psum.tile([P, T], BF16, tag="bank")
                 for j in range(TOKEN_TILES):
                     nc.tensor.transpose(
                         mem_bank[:, j * P : (j + 1) * P], mem_rows[:, j, ct * P : (ct + 1) * P], ident_bf16[:]
                     )
-                nc.vector.tensor_scalar_mul(out=neg_quarter_mem[ct][:], in0=mem_bank[:], scalar1=-0.25)
+                nc.vector.tensor_scalar_mul(out=quarter_mem[ct][:], in0=mem_bank[:], scalar1=0.25)
 
-        neg_quarter_means = {}
+        quarter_means = {}
+        mean_of_means = keep.tile([P, CHANNEL_TILES], F32)
 
         def token_mean(b):
             sums = plain_psum.tile([P, CHANNEL_TILES, MEAN_COLS], F32, tag="bank")
@@ -174,43 +187,49 @@ def tile_dynamicmemorybank_pb_kernel(tc, h, x, memory, w2_words, w2_scales, b2, 
                         start=(j == 0),
                         stop=(j == TOKEN_TILES - 1),
                     )
-            neg_quarter_mean = keep.tile([P, CHANNEL_TILES], F32, name="neg_quarter_mean_%d" % b)
-            nc.vector.tensor_copy(out=neg_quarter_mean[:], in_=sums[:, :, 0])
-            neg_quarter_means[b] = neg_quarter_mean
+            quarter_mean = keep.tile([P, CHANNEL_TILES], F32, name="quarter_mean_%d" % b)
+            nc.vector.tensor_copy(out=quarter_mean[:], in_=sums[:, :, 0])
+            quarter_means[b] = quarter_mean
+            if b == 0:
+                nc.vector.tensor_copy(out=mean_of_means[:], in_=sums[:, :, 0])
+            else:
+                nc.vector.tensor_tensor(out=mean_of_means[:], in0=sums[:, :, 0], in1=mean_of_means[:], op=ALU.add)
 
         blended = [keep.tile([P, T], F32, name="blended_%d" % ct) for ct in range(CHANNEL_TILES)]
 
         def gate_and_blend(b, ct, product):
-            gate = gates.tile([P, T], F32)
+            keep_gate = gates.tile([P, T], F32)
             nc.scalar.activation(
-                out=gate[:], in_=product[:], func=ACT.Sigmoid, bias=bias[:, ct : ct + 1], scale=1.0
+                out=keep_gate[:], in_=product[:], func=ACT.Sigmoid, bias=neg_bias[:, ct : ct + 1], scale=-1.0
             )
-            pull = gates.tile([P, T], F32)
+            pull = blended[ct] if b == 0 else gates.tile([P, T], F32, name="pull")
             nc.vector.scalar_tensor_tensor(
                 out=pull[:],
-                in0=neg_quarter_mem[ct][:],
-                scalar=neg_quarter_means[b][:, ct : ct + 1],
-                in1=gate[:],
+                in0=quarter_mem[ct][:],
+                scalar=quarter_means[b][:, ct : ct + 1],
+                in1=keep_gate[:],
                 op0=ALU.subtract,
                 op1=ALU.mult,
             )
-            if b == 0:
+            if 0 < b < B - 1:
+                nc.vector.tensor_tensor(out=blended[ct][:], in0=blended[ct][:], in1=pull[:], op=ALU.add)
+            if b == B - 1:
                 nc.vector.scalar_tensor_tensor(
                     out=blended[ct][:],
-                    in0=neg_quarter_mem[ct][:],
-                    scalar=-4.0,
-                    in1=pull[:],
-                    op0=ALU.mult,
+                    in0=pull[:],
+                    scalar=mean_of_means[:, ct : ct + 1],
+                    in1=blended[ct][:],
+                    op0=ALU.add,
                     op1=ALU.add,
                 )
-            else:
-                nc.vector.tensor_tensor(out=blended[ct][:], in0=blended[ct][:], in1=pull[:], op=ALU.add)
 
         for step in range(STEPS_PER_BATCH):
             quantise(step, transpose(step))
         for b in range(B):
             for run in range(STEPS_PER_BATCH):
                 ahead = (b + 1) * STEPS_PER_BATCH + run
+                if ahead + 1 < STEPS:
+                    regroup(ahead + 1)
                 if ahead < STEPS:
                     grouped = transpose(ahead)
                     if run == STEPS_PER_BATCH - 1:

@@ -22,6 +22,7 @@ TOKEN_TILES = T // P
 CHANNEL_TILES = C // P
 STEP_TILES = 2
 STEP_TOKENS = STEP_TILES * P
+REGROUPED_TILES = 1
 STEPS_PER_BATCH = TOKEN_TILES // STEP_TILES
 STEPS = B * STEPS_PER_BATCH
 LEAD = STEPS_PER_BATCH + 1
@@ -38,7 +39,7 @@ def tile_dynamicmemorybank_pb_kernel(tc, h, x, memory, w2_words, w2_scales, b2, 
     with ExitStack() as ctx:
         keep = ctx.enter_context(tc.tile_pool(name="keep", bufs=1))
         stage = ctx.enter_context(tc.tile_pool(name="stage", bufs=2))
-        ordered = ctx.enter_context(tc.tile_pool(name="ordered", bufs=2 * STEP_TILES))
+        ordered = ctx.enter_context(tc.tile_pool(name="ordered", bufs=2 * REGROUPED_TILES))
         mx_h = ctx.enter_context(tc.tile_pool(name="mx_h", bufs=2))
         gates = ctx.enter_context(tc.tile_pool(name="gates", bufs=4))
         mx_psum = ctx.enter_context(tc.psum_pool(name="mx_psum", bufs=2))
@@ -97,7 +98,7 @@ def tile_dynamicmemorybank_pb_kernel(tc, h, x, memory, w2_words, w2_scales, b2, 
         regrouped = {}
 
         def regroup(step):
-            for j in range(STEP_TILES):
+            for j in range(REGROUPED_TILES):
                 by_half = ordered.tile([P, PASSES, 2, P], F32, name="by_half")
                 nc.vector.tensor_copy(
                     out=by_half[:],

@@ -29,6 +29,7 @@ LEAD = STEPS_PER_BATCH + 1
 RUN_TILES = CHANNEL_TILES // STEPS_PER_BATCH
 BANK_PASSES = 2
 WORDS_PER_PASS = K_PASS // 2
+LAST_PIECES = 2
 MEAN_COLS = 32
 
 FLOPS = 2 * B * T * F * C
@@ -199,30 +200,39 @@ def tile_dynamicmemorybank_pb_kernel(tc, h, x, memory, w2_words, w2_scales, b2, 
         blended = [keep.tile([P, T], F32, name="blended_%d" % ct) for ct in range(CHANNEL_TILES)]
 
         def gate_and_blend(b, ct, product):
+            pieces = LAST_PIECES if (b, ct) == (B - 1, CHANNEL_TILES - 1) else 1
             keep_gate = gates.tile([P, T], F32)
-            nc.scalar.activation(
-                out=keep_gate[:], in_=product[:], func=ACT.Sigmoid, bias=neg_bias[:, ct : ct + 1], scale=-1.0
-            )
             pull = blended[ct] if b == 0 else gates.tile([P, T], F32, name="pull")
-            nc.vector.scalar_tensor_tensor(
-                out=pull[:],
-                in0=quarter_mem[ct][:],
-                scalar=quarter_means[b][:, ct : ct + 1],
-                in1=keep_gate[:],
-                op0=ALU.subtract,
-                op1=ALU.mult,
-            )
+            slices = [slice(i * T // pieces, (i + 1) * T // pieces) for i in range(pieces)]
+            for tokens in slices:
+                nc.scalar.activation(
+                    out=keep_gate[:, tokens],
+                    in_=product[:, tokens],
+                    func=ACT.Sigmoid,
+                    bias=neg_bias[:, ct : ct + 1],
+                    scale=-1.0,
+                )
+            for tokens in slices:
+                nc.vector.scalar_tensor_tensor(
+                    out=pull[:, tokens],
+                    in0=quarter_mem[ct][:, tokens],
+                    scalar=quarter_means[b][:, ct : ct + 1],
+                    in1=keep_gate[:, tokens],
+                    op0=ALU.subtract,
+                    op1=ALU.mult,
+                )
             if 0 < b < B - 1:
                 nc.vector.tensor_tensor(out=blended[ct][:], in0=blended[ct][:], in1=pull[:], op=ALU.add)
             if b == B - 1:
-                nc.vector.scalar_tensor_tensor(
-                    out=blended[ct][:],
-                    in0=pull[:],
-                    scalar=mean_of_means[:, ct : ct + 1],
-                    in1=blended[ct][:],
-                    op0=ALU.add,
-                    op1=ALU.add,
-                )
+                for tokens in slices:
+                    nc.vector.scalar_tensor_tensor(
+                        out=blended[ct][:, tokens],
+                        in0=pull[:, tokens],
+                        scalar=mean_of_means[:, ct : ct + 1],
+                        in1=blended[ct][:, tokens],
+                        op0=ALU.add,
+                        op1=ALU.add,
+                    )
 
         for step in range(STEPS_PER_BATCH):
             quantise(step, transpose(step))
@@ -247,9 +257,12 @@ def tile_dynamicmemorybank_pb_kernel(tc, h, x, memory, w2_words, w2_scales, b2, 
         out_rows = keep.tile([P, TOKEN_TILES, C], F32)
         out_by_tile = out[0].rearrange("(j p) c -> p j c", p=P)
         for ct in range(CHANNEL_TILES):
-            back = plain_psum.tile([P, TOKEN_TILES, P], F32, tag="bank")
-            for j in range(TOKEN_TILES):
-                nc.tensor.transpose(back[:, j, :], blended[ct][:, j * P : (j + 1) * P], ident_f32[:])
+            pieces = LAST_PIECES if ct == CHANNEL_TILES - 1 else 1
             channels = slice(ct * P, (ct + 1) * P)
-            nc.scalar.copy(out=out_rows[:, :, channels], in_=back[:])
-            nc.sync.dma_start(out=out_by_tile[:, :, channels], in_=out_rows[:, :, channels])
+            for i in range(pieces):
+                tiles = slice(i * TOKEN_TILES // pieces, (i + 1) * TOKEN_TILES // pieces)
+                back = plain_psum.tile([P, TOKEN_TILES, P], F32, tag="bank")
+                for j in range(tiles.start, tiles.stop):
+                    nc.tensor.transpose(back[:, j, :], blended[ct][:, j * P : (j + 1) * P], ident_f32[:])
+                nc.scalar.copy(out=out_rows[:, tiles, channels], in_=back[:, tiles, :])
+                nc.sync.dma_start(out=out_by_tile[:, tiles, channels], in_=out_rows[:, tiles, channels])

@@ -97,6 +97,7 @@ def tile_dynamicmemorybank_pb_kernel(tc, h, x, memory, w2_words, w2_scales, b2, 
                 load_x(step // STEPS_PER_BATCH)
 
         regrouped = {}
+        regrouped_steps = []
 
         def regroup(step):
             for j in range(REGROUPED_TILES):
@@ -106,28 +107,39 @@ def tile_dynamicmemorybank_pb_kernel(tc, h, x, memory, w2_words, w2_scales, b2, 
                     in_=h_tiles[(step, j)][:].bitcast(F32).rearrange("p (g m u) -> p g u m", g=PASSES, u=2),
                 )
                 regrouped[(step, j)] = by_half
+            regrouped_steps.append(step)
+
+        def pass_words(step, j, g, u):
+            if (step, j) in regrouped:
+                return regrouped[(step, j)][:, g, u, :]
+            return h_tiles[(step, j)][:].bitcast(F32)[:, g * WORDS_PER_PASS + u : (g + 1) * WORDS_PER_PASS : 2]
 
         def transpose(step):
             grouped = stage.tile([P, PASSES, PACK * STEP_TOKENS], BF16, align_bytes=64)
             grouped_words = grouped[:].bitcast(F32)
-            for j in range(STEP_TILES):
-                h_words = h_tiles[(step, j)][:].bitcast(F32)
-                for first_pass in range(0, PASSES, BANK_PASSES):
-                    bank = plain_psum.tile([P, BANK_PASSES, 2, P], F32, tag="bank")
-                    for i in range(BANK_PASSES):
-                        g = first_pass + i
-                        for u in range(2):
-                            if (step, j) in regrouped:
-                                words = regrouped[(step, j)][:, g, u, :]
-                            else:
-                                words = h_words[:, g * WORDS_PER_PASS + u : (g + 1) * WORDS_PER_PASS : 2]
-                            nc.tensor.transpose(bank[:, i, u, :], words, ident_f32[:])
+            if step in regrouped_steps:
+                for g in range(PASSES):
+                    bank = plain_psum.tile([P, STEP_TILES, 2, P], F32, tag="bank")
+                    for u in range(2):
+                        for j in range(STEP_TILES):
+                            nc.tensor.transpose(bank[:, j, u, :], pass_words(step, j, g, u), ident_f32[:])
                     nc.scalar.copy(
-                        out=grouped_words[
-                            :, first_pass : first_pass + BANK_PASSES, j * 2 * P : (j + 1) * 2 * P
-                        ].rearrange("p g (m u) -> p g m u", u=2),
-                        in_=bank[:].rearrange("p g u m -> p g m u"),
+                        out=grouped_words[:, g, :].rearrange("p (j m u) -> p j m u", j=STEP_TILES, u=2),
+                        in_=bank[:].rearrange("p j u m -> p j m u"),
                     )
+            else:
+                for j in range(STEP_TILES):
+                    for first_pass in range(0, PASSES, BANK_PASSES):
+                        bank = plain_psum.tile([P, BANK_PASSES, 2, P], F32, tag="bank")
+                        for i in range(BANK_PASSES):
+                            for u in range(2):
+                                nc.tensor.transpose(bank[:, i, u, :], pass_words(step, j, first_pass + i, u), ident_f32[:])
+                        nc.scalar.copy(
+                            out=grouped_words[
+                                :, first_pass : first_pass + BANK_PASSES, j * 2 * P : (j + 1) * 2 * P
+                            ].rearrange("p g (m u) -> p g m u", u=2),
+                            in_=bank[:].rearrange("p g u m -> p g m u"),
+                        )
             return grouped
 
         quantised = {}

from contextlib import ExitStack

import concourse.mybir as mybir
from concourse.masks import make_identity

F32 = mybir.dt.float32
BF16 = mybir.dt.bfloat16
I32 = mybir.dt.int32
U32 = mybir.dt.uint32
U8 = mybir.dt.uint8
FP8X4 = mybir.dt.float8_e4m3fn_x4
FP4X4 = mybir.dt.float4_e2m1fn_x4
ALU = mybir.AluOpType
ACT = mybir.ActivationFunctionType

B, T, C, F = 4, 512, 512, 2048
P = 128
PACK = 4
K_PASS = P * PACK
PASSES = F // K_PASS
TOKEN_TILES = T // P
CHANNEL_TILES = C // P
STEP_TILES = 2
STEP_TOKENS = STEP_TILES * P
REGROUPED_TILES = 1
STEPS_PER_BATCH = TOKEN_TILES // STEP_TILES
STEPS = B * STEPS_PER_BATCH
LEAD = STEPS_PER_BATCH + 1
RUN_TILES = CHANNEL_TILES // STEPS_PER_BATCH
BANK_PASSES = 2
WORDS_PER_PASS = K_PASS // 2
LAST_PIECES = 2
MEAN_COLS = 32

FLOPS = 2 * B * T * F * C


def tile_dynamicmemorybank_pb_kernel(tc, h, x, memory, w2_words, w2_scales, b2, out):
    nc = tc.nc
    with ExitStack() as ctx:
        keep = ctx.enter_context(tc.tile_pool(name="keep", bufs=1))
        stage = ctx.enter_context(tc.tile_pool(name="stage", bufs=2))
        ordered = ctx.enter_context(tc.tile_pool(name="ordered", bufs=2 * REGROUPED_TILES))
        mx_h = ctx.enter_context(tc.tile_pool(name="mx_h", bufs=2))
        gates = ctx.enter_context(tc.tile_pool(name="gates", bufs=4))
        mx_psum = ctx.enter_context(tc.psum_pool(name="mx_psum", bufs=2))
        plain_psum = ctx.enter_context(tc.psum_pool(name="plain_psum", bufs=6))

        ident_f32 = keep.tile([P, P], F32)
        make_identity(nc, ident_f32[:])
        ident_bf16 = keep.tile([P, P], BF16)
        make_identity(nc, ident_bf16[:])
        w_scales = keep.tile([P, PASSES, C], U8, align_bytes=64)
        nc.vector.memset(w_scales[:].bitcast(I32), 0)
        bias_rows = keep.tile([P, P], BF16)
        nc.vector.memset(bias_rows[:], 0.0)
        mean_weight = keep.tile([P, MEAN_COLS], BF16)
        nc.vector.memset(mean_weight[:], 1.0 / (B * T))
        table_warmer = keep.tile([P, 1], F32)
        nc.vector.memset(table_warmer[:], 0.0)
        nc.scalar.activation(out=table_warmer[:], in_=table_warmer[:], func=ACT.Sigmoid)

        h_tiles = {}

        def load_h(step):
            b, half = divmod(step, STEPS_PER_BATCH)
            for j in range(STEP_TILES):
                first_token = (half * STEP_TILES + j) * P
                h_tile = keep.tile([P, F], BF16, name="h_%d_%d" % (step, j))
                nc.sync.dma_start(out=h_tile[:], in_=h[b, first_token : first_token + P, :])
                h_tiles[(step, j)] = h_tile

        x_tiles = {}

        def load_x(b):
            x_tile = keep.tile([P, TOKEN_TILES, C], BF16, name="x_%d" % b)
            nc.sync.dma_start(
                out=x_tile[:].rearrange("p j c -> p (j c)"),
                in_=x[b].rearrange("(p j) c -> p (j c)", j=TOKEN_TILES),
            )
            x_tiles[b] = x_tile

        for step in range(LEAD):
            load_h(step)
        scale_rows = w2_scales.bitcast(I32).rearrange("g (Q r) n -> r Q g n", r=4)
        for r in range(4):
            nc.sync.dma_start(out=w_scales[r:P:32, :, :].bitcast(I32), in_=scale_rows[r])
        w_words = keep.tile([P, PASSES, 2 * C], U8, align_bytes=64)
        nc.sync.dma_start(out=w_words[:].bitcast(I32), in_=w2_words.bitcast(I32).rearrange("g p n -> p g n"))
        nc.sync.dma_start(out=bias_rows[0:CHANNEL_TILES, :], in_=b2.rearrange("(r c) -> r c", c=P))
        mem_rows = keep.tile([P, TOKEN_TILES, C], BF16)
        nc.sync.dma_start(out=mem_rows[:], in_=memory[0].rearrange("(j p) c -> p j c", p=P))
        load_x(0)
        for step in range(LEAD, STEPS):
            load_h(step)
            if step % STEPS_PER_BATCH == STEPS_PER_BATCH - 1:
                load_x(step // STEPS_PER_BATCH)

        regrouped = {}
        regrouped_steps = []

        def regroup(step):
            for j in range(REGROUPED_TILES):
                by_half = ordered.tile([P, PASSES, 2, P], F32, name="by_half")
                nc.vector.tensor_copy(
                    out=by_half[:],
                    in_=h_tiles[(step, j)][:].bitcast(F32).rearrange("p (g m u) -> p g u m", g=PASSES, u=2),
                )
                regrouped[(step, j)] = by_half
            regrouped_steps.append(step)

        def pass_words(step, j, g, u):
            if (step, j) in regrouped:
                return regrouped[(step, j)][:, g, u, :]
            return h_tiles[(step, j)][:].bitcast(F32)[:, g * WORDS_PER_PASS + u : (g + 1) * WORDS_PER_PASS : 2]

        def transpose(step):
            grouped = stage.tile([P, PASSES, PACK * STEP_TOKENS], BF16, align_bytes=64)
            grouped_words = grouped[:].bitcast(F32)
            if step in regrouped_steps:
                for g in range(PASSES):
                    bank = plain_psum.tile([P, STEP_TILES, 2, P], F32, tag="bank")
                    for u in range(2):
                        for j in range(STEP_TILES):
                            nc.tensor.transpose(bank[:, j, u, :], pass_words(step, j, g, u), ident_f32[:])
                    nc.scalar.copy(
                        out=grouped_words[:, g, :].rearrange("p (j m u) -> p j m u", j=STEP_TILES, u=2),
                        in_=bank[:].rearrange("p j u m -> p j m u"),
                    )
            else:
                for j in range(STEP_TILES):
                    for first_pass in range(0, PASSES, BANK_PASSES):
                        bank = plain_psum.tile([P, BANK_PASSES, 2, P], F32, tag="bank")
                        for i in range(BANK_PASSES):
                            for u in range(2):
                                nc.tensor.transpose(bank[:, i, u, :], pass_words(step, j, first_pass + i, u), ident_f32[:])
                        nc.scalar.copy(
                            out=grouped_words[
                                :, first_pass : first_pass + BANK_PASSES, j * 2 * P : (j + 1) * 2 * P
                            ].rearrange("p g (m u) -> p g m u", u=2),
                            in_=bank[:].rearrange("p g u m -> p g m u"),
                        )
            return grouped

        quantised = {}

        def quantise(step, grouped):
            b, half = divmod(step, STEPS_PER_BATCH)
            if half == 0:
                h_codes = mx_h.tile([P, PASSES, T], U32, align_bytes=64)
                h_scales = mx_h.tile([P, PASSES, T], U8, align_bytes=64)
                quantised[b] = (h_codes, h_scales)
            h_codes, h_scales = quantised[b]
            tokens = slice(half * STEP_TOKENS, (half + 1) * STEP_TOKENS)
            for g in range(PASSES):
                nc.vector.quantize_mx(
                    out=h_codes[:, g, tokens].bitcast(FP8X4), scales=h_scales[:, g, tokens], in_=grouped[:, g, :]
                )

        def multiply(b, ct):
            product = mx_psum.tile([P, T], F32)
            h_codes, h_scales = quantised[b]
            for g in range(PASSES):
                nc.tensor.matmul_mx(
                    out=product[:],
                    lhsT=w_words[:, g, ct * 2 * P : (ct + 1) * 2 * P].bitcast(FP4X4),
                    lhsT_scale=w_scales[:, g, ct * P : (ct + 1) * P],
                    rhs=h_codes[:, g, :].bitcast(FP8X4),
                    rhs_scale=h_scales[:, g, :],
                    start=(g == 0),
                    stop=(g == PASSES - 1),
                )
            return product

        neg_bias = keep.tile([P, CHANNEL_TILES], F32)
        quarter_mem = [keep.tile([P, T], BF16, name="quarter_mem_%d" % ct) for ct in range(CHANNEL_TILES)]

        def transpose_bias_and_memory():
            bias_bank = plain_psum.tile([P, P], BF16, tag="bank")
            nc.tensor.transpose(bias_bank[:], bias_rows[:], ident_bf16[:])
            nc.vector.tensor_scalar_mul(out=neg_bias[:], in0=bias_bank[:, 0:CHANNEL_TILES], scalar1=-1.0)
            for ct in range(CHANNEL_TILES):
                mem_bank = plain_psum.tile([P, T], BF16, tag="bank")
                for j in range(TOKEN_TILES):
                    nc.tensor.transpose(
                        mem_bank[:, j * P : (j + 1) * P], mem_rows[:, j, ct * P : (ct + 1) * P], ident_bf16[:]
                    )
                nc.vector.tensor_scalar_mul(out=quarter_mem[ct][:], in0=mem_bank[:], scalar1=0.25)

        quarter_means = {}
        mean_of_means = keep.tile([P, CHANNEL_TILES], F32)

        def token_mean(b):
            sums = plain_psum.tile([P, CHANNEL_TILES, MEAN_COLS], F32, tag="bank")
            for ct in range(CHANNEL_TILES):
                for j in range(TOKEN_TILES):
                    nc.tensor.matmul(
                        out=sums[:, ct, :],
                        lhsT=x_tiles[b][:, j, ct * P : (ct + 1) * P],
                        rhs=mean_weight[:],
                        start=(j == 0),
                        stop=(j == TOKEN_TILES - 1),
                    )
            quarter_mean = keep.tile([P, CHANNEL_TILES], F32, name="quarter_mean_%d" % b)
            nc.vector.tensor_copy(out=quarter_mean[:], in_=sums[:, :, 0])
            quarter_means[b] = quarter_mean
            if b == 0:
                nc.vector.tensor_copy(out=mean_of_means[:], in_=sums[:, :, 0])
            else:
                nc.vector.tensor_tensor(out=mean_of_means[:], in0=sums[:, :, 0], in1=mean_of_means[:], op=ALU.add)

        blended = [keep.tile([P, T], F32, name="blended_%d" % ct) for ct in range(CHANNEL_TILES)]

        def gate_and_blend(b, ct, product):
            pieces = LAST_PIECES if (b, ct) == (B - 1, CHANNEL_TILES - 1) else 1
            keep_gate = gates.tile([P, T], F32)
            pull = blended[ct] if b == 0 else gates.tile([P, T], F32, name="pull")
            slices = [slice(i * T // pieces, (i + 1) * T // pieces) for i in range(pieces)]
            for tokens in slices:
                nc.scalar.activation(
                    out=keep_gate[:, tokens],
                    in_=product[:, tokens],
                    func=ACT.Sigmoid,
                    bias=neg_bias[:, ct : ct + 1],
                    scale=-1.0,
                )
            for tokens in slices:
                nc.vector.scalar_tensor_tensor(
                    out=pull[:, tokens],
                    in0=quarter_mem[ct][:, tokens],
                    scalar=quarter_means[b][:, ct : ct + 1],
                    in1=keep_gate[:, tokens],
                    op0=ALU.subtract,
                    op1=ALU.mult,
                )
            if 0 < b < B - 1:
                nc.vector.tensor_tensor(out=blended[ct][:], in0=blended[ct][:], in1=pull[:], op=ALU.add)
            if b == B - 1:
                for tokens in slices:
                    nc.vector.scalar_tensor_tensor(
                        out=blended[ct][:, tokens],
                        in0=pull[:, tokens],
                        scalar=mean_of_means[:, ct : ct + 1],
                        in1=blended[ct][:, tokens],
                        op0=ALU.add,
                        op1=ALU.add,
                    )

        for step in range(STEPS_PER_BATCH):
            quantise(step, transpose(step))
        for b in range(B):
            for run in range(STEPS_PER_BATCH):
                ahead = (b + 1) * STEPS_PER_BATCH + run
                if ahead + 1 < STEPS:
                    regroup(ahead + 1)
                if ahead < STEPS:
                    grouped = transpose(ahead)
                    if run == STEPS_PER_BATCH - 1:
                        token_mean(b + 1)
                    quantise(ahead, grouped)
                tiles = range(run * RUN_TILES, (run + 1) * RUN_TILES)
                products = [multiply(b, ct) for ct in tiles]
                if b == 0 and run == 0:
                    transpose_bias_and_memory()
                    token_mean(0)
                for ct, product in zip(tiles, products):
                    gate_and_blend(b, ct, product)

        out_rows = keep.tile([P, TOKEN_TILES, C], F32)
        out_by_tile = out[0].rearrange("(j p) c -> p j c", p=P)
        for ct in range(CHANNEL_TILES):
            pieces = LAST_PIECES if ct == CHANNEL_TILES - 1 else 1
            channels = slice(ct * P, (ct + 1) * P)
            for i in range(pieces):
                tiles = slice(i * TOKEN_TILES // pieces, (i + 1) * TOKEN_TILES // pieces)
                back = plain_psum.tile([P, TOKEN_TILES, P], F32, tag="bank")
                for j in range(tiles.start, tiles.stop):
                    nc.tensor.transpose(back[:, j, :], blended[ct][:, j * P : (j + 1) * P], ident_f32[:])
                nc.scalar.copy(out=out_rows[:, tiles, channels], in_=back[:, tiles, :])
                nc.sync.dma_start(out=out_by_tile[:, tiles, channels], in_=out_rows[:, tiles, channels])
